import numpy as np
import ml_dtypes

BF16 = ml_dtypes.bfloat16


def bf(x):
    return np.asarray(x, np.float32).astype(BF16)


def f32(x):
    return np.asarray(x, np.float32)


def f64(x):
    return np.asarray(x).astype(np.float64)


def striped(idx):
    return np.tile(idx.reshape(-1, 16).T, (8, 1))


E, E2, V, N = 256, 512, 1024, 512


def setup_inputs():
    return {"emb": f32(np.random.standard_normal((E, V))), "lab": f32(np.tile(np.random.standard_normal((1, N)) > 0.0, (E, 1))), "w_in": bf(np.random.standard_normal((E2, E)) / np.sqrt(E)), "b_in": f32(0.1 * np.random.standard_normal((E, 1))), "offs": striped(np.random.permutation(np.tile(np.arange(V), 2))[:N])}


def reference(emb, lab, w_in, b_in, offs):
    idx = offs[:16].T.reshape(-1)
    e = f64(emb)[:, idx]
    a = f64(lab)
    cat = np.concatenate([e * a, e * (1.0 - a)], axis=0)
    return np.maximum(f64(w_in).T @ cat + f64(b_in), 0.0)

@@ -1,0 +1,67 @@
+import concourse.mybir as mybir
+
+F32, BF16, U16 = mybir.dt.float32, mybir.dt.bfloat16, mybir.dt.uint16
+MULT = mybir.AluOpType.mult
+COPY, RELU = mybir.ActivationFunctionType.Copy, mybir.ActivationFunctionType.Relu
+
+P = 128
+FLOPS = 2 * 512 * 256 * 512
+
+
+def tile_rkt_kernel(tc, emb, lab, w_in, b_in, offs, out):
+    nc = tc.nc
+    channels, items = emb.shape
+    entries = lab.shape[1]
+    features = out.shape[0]
+    channel_blocks = channels // P
+    feature_blocks = features // P
+    w_blocks = w_in.shape[0] // P
+
+    with tc.tile_pool(name="held", bufs=1) as held, tc.psum_pool(name="psum", bufs=1) as psum:
+        offsets = held.tile([P, entries // 16], U16, name="offsets")
+        nc.sync.dma_start(offsets[:], offs)
+
+        emb_tiles, lab_tiles = [], []
+        for c in range(channel_blocks):
+            emb_tile = held.tile([P, items], F32, name=f"emb{c}")
+            nc.sync.dma_start(emb_tile[:], emb[c * P : (c + 1) * P, :])
+            emb_tiles.append(emb_tile)
+            lab_tile = held.tile([P, entries], F32, name=f"lab{c}")
+            nc.scalar.dma_start(lab_tile[:], lab[c * P : (c + 1) * P, :])
+            lab_tiles.append(lab_tile)
+
+        w_tile = held.tile([P, w_blocks, features], BF16, name="w_tile")
+        nc.gpsimd.dma_start(w_tile[:], w_in.rearrange("(k p) m -> p k m", p=P))
+        bias_tiles = []
+        for m in range(feature_blocks):
+            bias_tile = held.tile([P, 1], F32, name=f"bias{m}")
+            nc.gpsimd.dma_start(bias_tile[:], b_in[m * P : (m + 1) * P, :])
+            bias_tiles.append(bias_tile)
+
+        banks = [psum.tile([P, entries], F32, name=f"bank{m}") for m in range(feature_blocks)]
+
+        steps = [(c, wrong) for c in range(channel_blocks) for wrong in (False, True)]
+        for step, (c, wrong) in enumerate(steps):
+            if wrong:
+                factor = held.tile([P, entries], F32, name=f"not_lab{c}")
+                nc.scalar.activation(factor[:], lab_tiles[c][:], COPY, bias=1.0, scale=-1.0)
+            else:
+                factor = lab_tiles[c]
+            product = held.tile([P, entries], F32, name=f"product{step}")
+            nc.vector.tensor_tensor(product[:], emb_tiles[c][:].indirect(offsets[:]), factor[:], MULT)
+            rounded = held.tile([P, entries], BF16, name=f"rounded{step}")
+            nc.scalar.copy(rounded[:], product[:])
+            k = c + channel_blocks if wrong else c
+            for m in range(feature_blocks):
+                nc.tensor.matmul(
+                    banks[m][:],
+                    w_tile[:, k, m * P : (m + 1) * P],
+                    rounded[:],
+                    start=(step == 0),
+                    stop=(step == len(steps) - 1),
+                )
+
+        for m in range(feature_blocks):
+            result = held.tile([P, entries], F32, name=f"result{m}")
+            nc.scalar.activation(result[:], banks[m][:], RELU, bias=bias_tiles[m][:])
+            nc.sync.dma_start(out[m * P : (m + 1) * P, :], result[:])

@@ -21,22 +21,22 @@ def tile_rkt_kernel(tc, emb, lab, w_in, b_in, offs, out):
         offsets = held.tile([P, entries // 16], U16, name="offsets")
         nc.sync.dma_start(offsets[:], offs)
 
-        emb_tiles, lab_tiles = [], []
-        for c in range(channel_blocks):
-            emb_tile = held.tile([P, items], F32, name=f"emb{c}")
-            nc.sync.dma_start(emb_tile[:], emb[c * P : (c + 1) * P, :])
-            emb_tiles.append(emb_tile)
-            lab_tile = held.tile([P, entries], F32, name=f"lab{c}")
-            nc.scalar.dma_start(lab_tile[:], lab[c * P : (c + 1) * P, :])
-            lab_tiles.append(lab_tile)
+        def load(tile, source):
+            nc.sync.dma_start(tile[: P // 2], source[: P // 2])
+            nc.scalar.dma_start(tile[P // 2 :], source[P // 2 :])
 
+        emb_tiles = [held.tile([P, items], F32, name=f"emb{c}") for c in range(channel_blocks)]
+        lab_tiles = [held.tile([P, entries], F32, name=f"lab{c}") for c in range(channel_blocks)]
         w_tile = held.tile([P, w_blocks, features], BF16, name="w_tile")
-        nc.gpsimd.dma_start(w_tile[:], w_in.rearrange("(k p) m -> p k m", p=P))
-        bias_tiles = []
+        bias_tiles = [held.tile([P, 1], F32, name=f"bias{m}") for m in range(feature_blocks)]
+
+        for c in range(channel_blocks):
+            load(lab_tiles[c], lab[c * P : (c + 1) * P, :])
+            load(emb_tiles[c], emb[c * P : (c + 1) * P, :])
+            if c == 0:
+                load(w_tile, w_in.rearrange("(k p) m -> p k m", p=P))
         for m in range(feature_blocks):
-            bias_tile = held.tile([P, 1], F32, name=f"bias{m}")
-            nc.gpsimd.dma_start(bias_tile[:], b_in[m * P : (m + 1) * P, :])
-            bias_tiles.append(bias_tile)
+            load(bias_tiles[m], b_in[m * P : (m + 1) * P, :])
 
         banks = [psum.tile([P, entries], F32, name=f"bank{m}") for m in range(feature_blocks)]
 

@@ -5,6 +5,7 @@ MULT = mybir.AluOpType.mult
 COPY, RELU = mybir.ActivationFunctionType.Copy, mybir.ActivationFunctionType.Relu
 
 P = 128
+PIECES = 2
 FLOPS = 2 * 512 * 256 * 512
 
 
@@ -16,52 +17,55 @@ def tile_rkt_kernel(tc, emb, lab, w_in, b_in, offs, out):
     channel_blocks = channels // P
     feature_blocks = features // P
     w_blocks = w_in.shape[0] // P
+    piece = entries // PIECES
 
     with tc.tile_pool(name="held", bufs=1) as held, tc.psum_pool(name="psum", bufs=1) as psum:
         offsets = held.tile([P, entries // 16], U16, name="offsets")
         nc.sync.dma_start(offsets[:], offs)
 
-        def load(tile, source):
-            nc.sync.dma_start(tile[: P // 2], source[: P // 2])
-            nc.scalar.dma_start(tile[P // 2 :], source[P // 2 :])
-
         emb_tiles = [held.tile([P, items], F32, name=f"emb{c}") for c in range(channel_blocks)]
         lab_tiles = [held.tile([P, entries], F32, name=f"lab{c}") for c in range(channel_blocks)]
         w_tile = held.tile([P, w_blocks, features], BF16, name="w_tile")
-        bias_tiles = [held.tile([P, 1], F32, name=f"bias{m}") for m in range(feature_blocks)]
 
         for c in range(channel_blocks):
-            load(lab_tiles[c], lab[c * P : (c + 1) * P, :])
-            load(emb_tiles[c], emb[c * P : (c + 1) * P, :])
+            nc.sync.dma_start(lab_tiles[c][:], lab[c * P : (c + 1) * P, :])
+            nc.sync.dma_start(emb_tiles[c][:], emb[c * P : (c + 1) * P, :])
             if c == 0:
-                load(w_tile, w_in.rearrange("(k p) m -> p k m", p=P))
+                nc.sync.dma_start(w_tile[:], w_in.rearrange("(k p) m -> p k m", p=P))
+
+        bias_tiles = []
         for m in range(feature_blocks):
-            load(bias_tiles[m], b_in[m * P : (m + 1) * P, :])
+            bias_tile = held.tile([P, 1], F32, name=f"bias{m}")
+            nc.gpsimd.dma_start(bias_tile[:], b_in[m * P : (m + 1) * P, :])
+            bias_tiles.append(bias_tile)
 
-        banks = [psum.tile([P, entries], F32, name=f"bank{m}") for m in range(feature_blocks)]
+        not_lab_tiles = []
+        for c in range(channel_blocks):
+            not_lab_tile = held.tile([P, entries], F32, name=f"not_lab{c}")
+            nc.scalar.activation(not_lab_tile[:], lab_tiles[c][:], COPY, bias=1.0, scale=-1.0)
+            not_lab_tiles.append(not_lab_tile)
 
-        steps = [(c, wrong) for c in range(channel_blocks) for wrong in (False, True)]
-        for step, (c, wrong) in enumerate(steps):
-            if wrong:
-                factor = held.tile([P, entries], F32, name=f"not_lab{c}")
-                nc.scalar.activation(factor[:], lab_tiles[c][:], COPY, bias=1.0, scale=-1.0)
-            else:
-                factor = lab_tiles[c]
-            product = held.tile([P, entries], F32, name=f"product{step}")
-            nc.vector.tensor_tensor(product[:], emb_tiles[c][:].indirect(offsets[:]), factor[:], MULT)
-            rounded = held.tile([P, entries], BF16, name=f"rounded{step}")
-            nc.scalar.copy(rounded[:], product[:])
-            k = c + channel_blocks if wrong else c
-            for m in range(feature_blocks):
-                nc.tensor.matmul(
-                    banks[m][:],
-                    w_tile[:, k, m * P : (m + 1) * P],
-                    rounded[:],
-                    start=(step == 0),
-                    stop=(step == len(steps) - 1),
-                )
+        banks = [[psum.tile([P, piece], F32, name=f"bank{m}_{h}") for h in range(PIECES)] for m in range(feature_blocks)]
 
-        for m in range(feature_blocks):
-            result = held.tile([P, entries], F32, name=f"result{m}")
-            nc.scalar.activation(result[:], banks[m][:], RELU, bias=bias_tiles[m][:])
-            nc.sync.dma_start(out[m * P : (m + 1) * P, :], result[:])
+        for c in range(channel_blocks):
+            for h in range(PIECES):
+                columns = slice(h * piece, (h + 1) * piece)
+                piece_offsets = offsets[:, h * piece // 16 : (h + 1) * piece // 16]
+                for k, factor in ((c, lab_tiles[c]), (channel_blocks + c, not_lab_tiles[c])):
+                    product = held.tile([P, piece], F32, name=f"product{k}_{h}")
+                    nc.vector.tensor_tensor(product[:], emb_tiles[c][:].indirect(piece_offsets), factor[:, columns], MULT)
+                    rounded = held.tile([P, piece], BF16, name=f"rounded{k}_{h}")
+                    nc.scalar.copy(rounded[:], product[:])
+                    for m in range(feature_blocks):
+                        nc.tensor.matmul(
+                            banks[m][h][:],
+                            w_tile[:, k, m * P : (m + 1) * P],
+                            rounded[:],
+                            start=(k == 0),
+                            stop=(k == w_blocks - 1),
+                        )
+                if c == channel_blocks - 1:
+                    for m in range(feature_blocks):
+                        result = held.tile([P, piece], F32, name=f"result{m}_{h}")
+                        nc.scalar.activation(result[:], banks[m][h][:], RELU, bias=bias_tiles[m][:])
+                        nc.sync.dma_start(out[m * P : (m + 1) * P, columns], result[:])

@@ -23,16 +23,17 @@ def tile_rkt_kernel(tc, emb, lab, w_in, b_in, offs, out):
         offsets = held.tile([P, entries // 16], U16, name="offsets")
         nc.sync.dma_start(offsets[:], offs)
 
-        emb_tiles = [held.tile([P, items], F32, name=f"emb{c}") for c in range(channel_blocks)]
-        lab_tiles = [held.tile([P, entries], F32, name=f"lab{c}") for c in range(channel_blocks)]
-        w_tile = held.tile([P, w_blocks, features], BF16, name="w_tile")
-
+        emb_tiles, lab_tiles = [], []
         for c in range(channel_blocks):
-            nc.sync.dma_start(lab_tiles[c][:], lab[c * P : (c + 1) * P, :])
-            nc.sync.dma_start(emb_tiles[c][:], emb[c * P : (c + 1) * P, :])
-            if c == 0:
-                nc.sync.dma_start(w_tile[:], w_in.rearrange("(k p) m -> p k m", p=P))
+            emb_tile = held.tile([P, items], F32, name=f"emb{c}")
+            nc.sync.dma_start(emb_tile[:], emb[c * P : (c + 1) * P, :])
+            emb_tiles.append(emb_tile)
+            lab_tile = held.tile([P, entries], F32, name=f"lab{c}")
+            nc.scalar.dma_start(lab_tile[:], lab[c * P : (c + 1) * P, :])
+            lab_tiles.append(lab_tile)
 
+        w_tile = held.tile([P, w_blocks, features], BF16, name="w_tile")
+        nc.gpsimd.dma_start(w_tile[:], w_in.rearrange("(k p) m -> p k m", p=P))
         bias_tiles = []
         for m in range(feature_blocks):
             bias_tile = held.tile([P, 1], F32, name=f"bias{m}")

@@ -23,22 +23,19 @@ def tile_rkt_kernel(tc, emb, lab, w_in, b_in, offs, out):
         offsets = held.tile([P, entries // 16], U16, name="offsets")
         nc.sync.dma_start(offsets[:], offs)
 
-        emb_tiles, lab_tiles = [], []
-        for c in range(channel_blocks):
-            emb_tile = held.tile([P, items], F32, name=f"emb{c}")
-            nc.sync.dma_start(emb_tile[:], emb[c * P : (c + 1) * P, :])
-            emb_tiles.append(emb_tile)
-            lab_tile = held.tile([P, entries], F32, name=f"lab{c}")
-            nc.scalar.dma_start(lab_tile[:], lab[c * P : (c + 1) * P, :])
-            lab_tiles.append(lab_tile)
-
+        emb_tiles = [held.tile([P, items], F32, name=f"emb{c}") for c in range(channel_blocks)]
+        lab_tiles = [held.tile([P, entries], F32, name=f"lab{c}") for c in range(channel_blocks)]
         w_tile = held.tile([P, w_blocks, features], BF16, name="w_tile")
-        nc.gpsimd.dma_start(w_tile[:], w_in.rearrange("(k p) m -> p k m", p=P))
-        bias_tiles = []
-        for m in range(feature_blocks):
-            bias_tile = held.tile([P, 1], F32, name=f"bias{m}")
-            nc.gpsimd.dma_start(bias_tile[:], b_in[m * P : (m + 1) * P, :])
-            bias_tiles.append(bias_tile)
+
+        for c in range(channel_blocks):
+            nc.sync.dma_start(lab_tiles[c][:], lab[c * P : (c + 1) * P, :])
+            nc.sync.dma_start(emb_tiles[c][:], emb[c * P : (c + 1) * P, :])
+            if c == 0:
+                nc.sync.dma_start(w_tile[:], w_in.rearrange("(k p) m -> p k m", p=P))
+
+        bias_tile = held.tile([P, feature_blocks], F32, name="bias_tile")
+        with nc.allow_non_contiguous_dma(reason="one 4-byte bias to a partition"):
+            nc.sync.dma_start(bias_tile[:], b_in.rearrange("(m p) one -> p (m one)", p=P))
 
         not_lab_tiles = []
         for c in range(channel_blocks):
@@ -68,5 +65,5 @@ def tile_rkt_kernel(tc, emb, lab, w_in, b_in, offs, out):
                 if c == channel_blocks - 1:
                     for m in range(feature_blocks):
                         result = held.tile([P, piece], F32, name=f"result{m}_{h}")
-                        nc.scalar.activation(result[:], banks[m][h][:], RELU, bias=bias_tiles[m][:])
+                        nc.scalar.activation(result[:], banks[m][h][:], RELU, bias=bias_tile[:, m : m + 1])
                         nc.sync.dma_start(out[m * P : (m + 1) * P, columns], result[:])

@@ -1,7 +1,7 @@
 import concourse.mybir as mybir
 
 F32, BF16, U16 = mybir.dt.float32, mybir.dt.bfloat16, mybir.dt.uint16
-MULT = mybir.AluOpType.mult
+MULT, ADD, MAX = mybir.AluOpType.mult, mybir.AluOpType.add, mybir.AluOpType.max
 COPY, RELU = mybir.ActivationFunctionType.Copy, mybir.ActivationFunctionType.Relu
 
 P = 128
@@ -53,7 +53,10 @@ def tile_rkt_kernel(tc, emb, lab, w_in, b_in, offs, out):
                     product = held.tile([P, piece], F32, name=f"product{k}_{h}")
                     nc.vector.tensor_tensor(product[:], emb_tiles[c][:].indirect(piece_offsets), factor[:, columns], MULT)
                     rounded = held.tile([P, piece], BF16, name=f"rounded{k}_{h}")
-                    nc.scalar.copy(rounded[:], product[:])
+                    if (c, h, k) == (channel_blocks - 1, PIECES - 1, w_blocks - 1):
+                        nc.vector.tensor_copy(rounded[:], product[:])
+                    else:
+                        nc.scalar.copy(rounded[:], product[:])
                     for m in range(feature_blocks):
                         nc.tensor.matmul(
                             banks[m][h][:],
@@ -65,5 +68,9 @@ def tile_rkt_kernel(tc, emb, lab, w_in, b_in, offs, out):
                 if c == channel_blocks - 1:
                     for m in range(feature_blocks):
                         result = held.tile([P, piece], F32, name=f"result{m}_{h}")
-                        nc.scalar.activation(result[:], banks[m][h][:], RELU, bias=bias_tile[:, m : m + 1])
-                        nc.sync.dma_start(out[m * P : (m + 1) * P, columns], result[:])
+                        if h == PIECES - 1 and m == 1:
+                            nc.vector.tensor_scalar(result[:], banks[m][h][:], bias_tile[:, m : m + 1], 0.0, ADD, MAX)
+                        else:
+                            nc.scalar.activation(result[:], banks[m][h][:], RELU, bias=bias_tile[:, m : m + 1])
+                        store_queue = nc.scalar if m == 0 else nc.sync
+                        store_queue.dma_start(out[m * P : (m + 1) * P, columns], result[:])

@@ -24,11 +24,11 @@ def tile_rkt_kernel(tc, emb, lab, w_in, b_in, offs, out):
         nc.sync.dma_start(offsets[:], offs)
 
         emb_tiles = [held.tile([P, items], F32, name=f"emb{c}") for c in range(channel_blocks)]
-        lab_tiles = [held.tile([P, entries], F32, name=f"lab{c}") for c in range(channel_blocks)]
+        lab_tile = held.tile([P, entries], F32, name="lab_tile")
         w_tile = held.tile([P, w_blocks, features], BF16, name="w_tile")
 
+        nc.sync.dma_start(lab_tile[:], lab[0:P, :])
         for c in range(channel_blocks):
-            nc.sync.dma_start(lab_tiles[c][:], lab[c * P : (c + 1) * P, :])
             nc.sync.dma_start(emb_tiles[c][:], emb[c * P : (c + 1) * P, :])
             if c == 0:
                 nc.sync.dma_start(w_tile[:], w_in.rearrange("(k p) m -> p k m", p=P))
@@ -37,11 +37,8 @@ def tile_rkt_kernel(tc, emb, lab, w_in, b_in, offs, out):
         with nc.allow_non_contiguous_dma(reason="one 4-byte bias to a partition"):
             nc.sync.dma_start(bias_tile[:], b_in.rearrange("(m p) one -> p (m one)", p=P))
 
-        not_lab_tiles = []
-        for c in range(channel_blocks):
-            not_lab_tile = held.tile([P, entries], F32, name=f"not_lab{c}")
-            nc.scalar.activation(not_lab_tile[:], lab_tiles[c][:], COPY, bias=1.0, scale=-1.0)
-            not_lab_tiles.append(not_lab_tile)
+        not_lab_tile = held.tile([P, entries], F32, name="not_lab_tile")
+        nc.scalar.activation(not_lab_tile[:], lab_tile[:], COPY, bias=1.0, scale=-1.0)
 
         banks = [[psum.tile([P, piece], F32, name=f"bank{m}_{h}") for h in range(PIECES)] for m in range(feature_blocks)]
 
@@ -49,7 +46,7 @@ def tile_rkt_kernel(tc, emb, lab, w_in, b_in, offs, out):
             for h in range(PIECES):
                 columns = slice(h * piece, (h + 1) * piece)
                 piece_offsets = offsets[:, h * piece // 16 : (h + 1) * piece // 16]
-                for k, factor in ((c, lab_tiles[c]), (channel_blocks + c, not_lab_tiles[c])):
+                for k, factor in ((c, lab_tile), (channel_blocks + c, not_lab_tile)):
                     product = held.tile([P, piece], F32, name=f"product{k}_{h}")
                     nc.vector.tensor_tensor(product[:], emb_tiles[c][:].indirect(piece_offsets), factor[:, columns], MULT)
                     rounded = held.tile([P, piece], BF16, name=f"rounded{k}_{h}")

@@ -5,7 +5,7 @@ MULT, ADD, MAX = mybir.AluOpType.mult, mybir.AluOpType.add, mybir.AluOpType.max
 COPY, RELU = mybir.ActivationFunctionType.Copy, mybir.ActivationFunctionType.Relu
 
 P = 128
-PIECES = 2
+PIECE_WIDTHS = (256, 128, 128)
 FLOPS = 2 * 512 * 256 * 512
 
 
@@ -17,7 +17,9 @@ def tile_rkt_kernel(tc, emb, lab, w_in, b_in, offs, out):
     channel_blocks = channels // P
     feature_blocks = features // P
     w_blocks = w_in.shape[0] // P
-    piece = entries // PIECES
+    assert sum(PIECE_WIDTHS) == entries
+    pieces = [(sum(PIECE_WIDTHS[:h]), width) for h, width in enumerate(PIECE_WIDTHS)]
+    last_piece = len(pieces) - 1
 
     with tc.tile_pool(name="held", bufs=1) as held, tc.psum_pool(name="psum", bufs=1) as psum:
         offsets = held.tile([P, entries // 16], U16, name="offsets")
@@ -26,48 +28,61 @@ def tile_rkt_kernel(tc, emb, lab, w_in, b_in, offs, out):
         emb_tiles = [held.tile([P, items], F32, name=f"emb{c}") for c in range(channel_blocks)]
         lab_tile = held.tile([P, entries], F32, name="lab_tile")
         w_tile = held.tile([P, w_blocks, features], BF16, name="w_tile")
+        bias_tile = held.tile([P, feature_blocks], F32, name="bias_tile")
 
         nc.sync.dma_start(lab_tile[:], lab[0:P, :])
-        for c in range(channel_blocks):
+        nc.sync.dma_start(emb_tiles[0][:], emb[0:P, :])
+        nc.sync.dma_start(w_tile[:], w_in.rearrange("(k p) m -> p k m", p=P))
+        for c in range(1, channel_blocks):
             nc.sync.dma_start(emb_tiles[c][:], emb[c * P : (c + 1) * P, :])
-            if c == 0:
-                nc.sync.dma_start(w_tile[:], w_in.rearrange("(k p) m -> p k m", p=P))
-
-        bias_tile = held.tile([P, feature_blocks], F32, name="bias_tile")
         with nc.allow_non_contiguous_dma(reason="one 4-byte bias to a partition"):
             nc.sync.dma_start(bias_tile[:], b_in.rearrange("(m p) one -> p (m one)", p=P))
 
         not_lab_tile = held.tile([P, entries], F32, name="not_lab_tile")
         nc.scalar.activation(not_lab_tile[:], lab_tile[:], COPY, bias=1.0, scale=-1.0)
 
-        banks = [[psum.tile([P, piece], F32, name=f"bank{m}_{h}") for h in range(PIECES)] for m in range(feature_blocks)]
+        banks = [[psum.tile([P, width], F32, name=f"bank{m}_{h}") for h, (first, width) in enumerate(pieces)] for m in range(feature_blocks)]
 
-        for c in range(channel_blocks):
-            for h in range(PIECES):
-                columns = slice(h * piece, (h + 1) * piece)
-                piece_offsets = offsets[:, h * piece // 16 : (h + 1) * piece // 16]
-                for k, factor in ((c, lab_tile), (channel_blocks + c, not_lab_tile)):
-                    product = held.tile([P, piece], F32, name=f"product{k}_{h}")
-                    nc.vector.tensor_tensor(product[:], emb_tiles[c][:].indirect(piece_offsets), factor[:, columns], MULT)
-                    rounded = held.tile([P, piece], BF16, name=f"rounded{k}_{h}")
-                    if (c, h, k) == (channel_blocks - 1, PIECES - 1, w_blocks - 1):
-                        nc.vector.tensor_copy(rounded[:], product[:])
-                    else:
-                        nc.scalar.copy(rounded[:], product[:])
-                    for m in range(feature_blocks):
-                        nc.tensor.matmul(
-                            banks[m][h][:],
-                            w_tile[:, k, m * P : (m + 1) * P],
-                            rounded[:],
-                            start=(k == 0),
-                            stop=(k == w_blocks - 1),
-                        )
-                if c == channel_blocks - 1:
-                    for m in range(feature_blocks):
-                        result = held.tile([P, piece], F32, name=f"result{m}_{h}")
-                        if h == PIECES - 1 and m == 1:
-                            nc.vector.tensor_scalar(result[:], banks[m][h][:], bias_tile[:, m : m + 1], 0.0, ADD, MAX)
-                        else:
-                            nc.scalar.activation(result[:], banks[m][h][:], RELU, bias=bias_tile[:, m : m + 1])
-                        store_queue = nc.scalar if m == 0 else nc.sync
-                        store_queue.dma_start(out[m * P : (m + 1) * P, columns], result[:])
+        def look_up_and_project(c, k, factor, first, width, piece_numbers):
+            product = held.tile([P, width], F32, name=f"product{k}_{first}")
+            nc.vector.tensor_tensor(
+                product[:],
+                emb_tiles[c][:].indirect(offsets[:, first // 16 : (first + width) // 16]),
+                factor[:, first : first + width],
+                MULT,
+            )
+            rounded = held.tile([P, width], BF16, name=f"rounded{k}_{first}")
+            if k == w_blocks - 1 and piece_numbers[-1] == last_piece:
+                nc.vector.tensor_copy(rounded[:], product[:])
+            else:
+                nc.scalar.copy(rounded[:], product[:])
+            for m in range(feature_blocks):
+                for h in piece_numbers:
+                    piece_first, piece_width = pieces[h]
+                    nc.tensor.matmul(
+                        banks[m][h][:],
+                        w_tile[:, k, m * P : (m + 1) * P],
+                        rounded[:, piece_first - first : piece_first - first + piece_width],
+                        start=(k == 0),
+                        stop=(k == w_blocks - 1),
+                    )
+
+        def finish(h, m):
+            first, width = pieces[h]
+            result = held.tile([P, width], F32, name=f"result{m}_{h}")
+            if (h, m) == (last_piece, 1):
+                nc.vector.tensor_scalar(result[:], banks[m][h][:], bias_tile[:, m : m + 1], 0.0, ADD, MAX)
+            else:
+                nc.scalar.activation(result[:], banks[m][h][:], RELU, bias=bias_tile[:, m : m + 1])
+            store_queue = nc.scalar if (h, m) == (last_piece, 0) else nc.sync
+            store_queue.dma_start(out[m * P : (m + 1) * P, first : first + width], result[:])
+
+        for c in range(channel_blocks - 1):
+            look_up_and_project(c, c, lab_tile, 0, entries, list(range(len(pieces))))
+            look_up_and_project(c, channel_blocks + c, not_lab_tile, 0, entries, list(range(len(pieces))))
+        c = channel_blocks - 1
+        for h, (first, width) in enumerate(pieces):
+            look_up_and_project(c, c, lab_tile, first, width, [h])
+            look_up_and_project(c, channel_blocks + c, not_lab_tile, first, width, [h])
+            for m in range(feature_blocks):
+                finish(h, m)

@@ -6,6 +6,7 @@ COPY, RELU = mybir.ActivationFunctionType.Copy, mybir.ActivationFunctionType.Rel
 
 P = 128
 PIECE_WIDTHS = (256, 128, 128)
+EARLY_WIDTH = 256
 FLOPS = 2 * 512 * 256 * 512
 
 
@@ -78,8 +79,10 @@ def tile_rkt_kernel(tc, emb, lab, w_in, b_in, offs, out):
             store_queue.dma_start(out[m * P : (m + 1) * P, first : first + width], result[:])
 
         for c in range(channel_blocks - 1):
-            look_up_and_project(c, c, lab_tile, 0, entries, list(range(len(pieces))))
-            look_up_and_project(c, channel_blocks + c, not_lab_tile, 0, entries, list(range(len(pieces))))
+            for early_first in range(0, entries, EARLY_WIDTH):
+                covered = [h for h, (first, width) in enumerate(pieces) if early_first <= first < early_first + EARLY_WIDTH]
+                look_up_and_project(c, c, lab_tile, early_first, EARLY_WIDTH, covered)
+                look_up_and_project(c, channel_blocks + c, not_lab_tile, early_first, EARLY_WIDTH, covered)
         c = channel_blocks - 1
         for h, (first, width) in enumerate(pieces):
             look_up_and_project(c, c, lab_tile, first, width, [h])

@@ -75,8 +75,7 @@ def tile_rkt_kernel(tc, emb, lab, w_in, b_in, offs, out):
                 nc.vector.tensor_scalar(result[:], banks[m][h][:], bias_tile[:, m : m + 1], 0.0, ADD, MAX)
             else:
                 nc.scalar.activation(result[:], banks[m][h][:], RELU, bias=bias_tile[:, m : m + 1])
-            store_queue = nc.scalar if (h, m) == (last_piece, 0) else nc.sync
-            store_queue.dma_start(out[m * P : (m + 1) * P, first : first + width], result[:])
+            nc.sync.dma_start(out[m * P : (m + 1) * P, first : first + width], result[:])
 
         for c in range(channel_blocks - 1):
             for early_first in range(0, entries, EARLY_WIDTH):

@@ -31,8 +31,9 @@ def tile_rkt_kernel(tc, emb, lab, w_in, b_in, offs, out):
         w_tile = held.tile([P, w_blocks, features], BF16, name="w_tile")
         bias_tile = held.tile([P, feature_blocks], F32, name="bias_tile")
 
-        nc.sync.dma_start(lab_tile[:], lab[0:P, :])
+        nc.sync.dma_start(lab_tile[:, 0:EARLY_WIDTH], lab[0:P, 0:EARLY_WIDTH])
         nc.sync.dma_start(emb_tiles[0][:], emb[0:P, :])
+        nc.sync.dma_start(lab_tile[:, EARLY_WIDTH:entries], lab[0:P, EARLY_WIDTH:entries])
         nc.sync.dma_start(w_tile[:], w_in.rearrange("(k p) m -> p k m", p=P))
         for c in range(1, channel_blocks):
             nc.sync.dma_start(emb_tiles[c][:], emb[c * P : (c + 1) * P, :])
@@ -40,7 +41,8 @@ def tile_rkt_kernel(tc, emb, lab, w_in, b_in, offs, out):
             nc.sync.dma_start(bias_tile[:], b_in.rearrange("(m p) one -> p (m one)", p=P))
 
         not_lab_tile = held.tile([P, entries], F32, name="not_lab_tile")
-        nc.scalar.activation(not_lab_tile[:], lab_tile[:], COPY, bias=1.0, scale=-1.0)
+        for columns in (slice(0, EARLY_WIDTH), slice(EARLY_WIDTH, entries)):
+            nc.scalar.activation(not_lab_tile[:, columns], lab_tile[:, columns], COPY, bias=1.0, scale=-1.0)
 
         banks = [[psum.tile([P, width], F32, name=f"bank{m}_{h}") for h, (first, width) in enumerate(pieces)] for m in range(feature_blocks)]
 

@@ -73,10 +73,10 @@ def tile_rkt_kernel(tc, emb, lab, w_in, b_in, offs, out):
         def finish(h, m):
             first, width = pieces[h]
             result = held.tile([P, width], F32, name=f"result{m}_{h}")
-            if (h, m) == (last_piece, 1):
-                nc.vector.tensor_scalar(result[:], banks[m][h][:], bias_tile[:, m : m + 1], 0.0, ADD, MAX)
-            else:
+            if m == 0:
                 nc.scalar.activation(result[:], banks[m][h][:], RELU, bias=bias_tile[:, m : m + 1])
+            else:
+                nc.vector.tensor_scalar(result[:], banks[m][h][:], bias_tile[:, m : m + 1], 0.0, ADD, MAX)
             nc.sync.dma_start(out[m * P : (m + 1) * P, first : first + width], result[:])
 
         for c in range(channel_blocks - 1):
@@ -88,5 +88,9 @@ def tile_rkt_kernel(tc, emb, lab, w_in, b_in, offs, out):
         for h, (first, width) in enumerate(pieces):
             look_up_and_project(c, c, lab_tile, first, width, [h])
             look_up_and_project(c, channel_blocks + c, not_lab_tile, first, width, [h])
-            for m in range(feature_blocks):
-                finish(h, m)
+            if h > 0:
+                finish(h - 1, 0)
+        for h in range(last_piece):
+            finish(h, 1)
+        for m in range(feature_blocks):
+            finish(last_piece, m)

@@ -6,7 +6,6 @@ COPY, RELU = mybir.ActivationFunctionType.Copy, mybir.ActivationFunctionType.Rel
 
 P = 128
 PIECE_WIDTHS = (256, 128, 128)
-EARLY_WIDTH = 256
 FLOPS = 2 * 512 * 256 * 512
 
 
@@ -27,21 +26,24 @@ def tile_rkt_kernel(tc, emb, lab, w_in, b_in, offs, out):
         nc.sync.dma_start(offsets[:], offs)
 
         emb_tiles = [held.tile([P, items], F32, name=f"emb{c}") for c in range(channel_blocks)]
+        emb_blocks = emb.rearrange("(p c) item -> c p item", c=channel_blocks)
         lab_tile = held.tile([P, entries], F32, name="lab_tile")
-        w_tile = held.tile([P, w_blocks, features], BF16, name="w_tile")
+        w_tile = held.tile([P, w_blocks // channel_blocks, channel_blocks, features], BF16, name="w_tile")
         bias_tile = held.tile([P, feature_blocks], F32, name="bias_tile")
 
-        nc.sync.dma_start(lab_tile[:, 0:EARLY_WIDTH], lab[0:P, 0:EARLY_WIDTH])
-        nc.sync.dma_start(emb_tiles[0][:], emb[0:P, :])
-        nc.sync.dma_start(lab_tile[:, EARLY_WIDTH:entries], lab[0:P, EARLY_WIDTH:entries])
-        nc.sync.dma_start(w_tile[:], w_in.rearrange("(k p) m -> p k m", p=P))
+        lab_loads = [slice(first, first + width) for first, width in [pieces[last_piece]] + pieces[:last_piece]]
+        nc.sync.dma_start(lab_tile[:, lab_loads[0]], lab[0:P, lab_loads[0]])
+        nc.sync.dma_start(emb_tiles[0][:], emb_blocks[0])
+        for columns in lab_loads[1:]:
+            nc.sync.dma_start(lab_tile[:, columns], lab[0:P, columns])
+        nc.sync.dma_start(w_tile[:], w_in.rearrange("(half p c) m -> p half c m", p=P, c=channel_blocks))
         for c in range(1, channel_blocks):
-            nc.sync.dma_start(emb_tiles[c][:], emb[c * P : (c + 1) * P, :])
+            nc.sync.dma_start(emb_tiles[c][:], emb_blocks[c])
         with nc.allow_non_contiguous_dma(reason="one 4-byte bias to a partition"):
             nc.sync.dma_start(bias_tile[:], b_in.rearrange("(m p) one -> p (m one)", p=P))
 
         not_lab_tile = held.tile([P, entries], F32, name="not_lab_tile")
-        for columns in (slice(0, EARLY_WIDTH), slice(EARLY_WIDTH, entries)):
+        for columns in lab_loads:
             nc.scalar.activation(not_lab_tile[:, columns], lab_tile[:, columns], COPY, bias=1.0, scale=-1.0)
 
         banks = [[psum.tile([P, width], F32, name=f"bank{m}_{h}") for h, (first, width) in enumerate(pieces)] for m in range(feature_blocks)]
@@ -64,7 +66,7 @@ def tile_rkt_kernel(tc, emb, lab, w_in, b_in, offs, out):
                     piece_first, piece_width = pieces[h]
                     nc.tensor.matmul(
                         banks[m][h][:],
-                        w_tile[:, k, m * P : (m + 1) * P],
+                        w_tile[:, k // channel_blocks, k % channel_blocks, m * P : (m + 1) * P],
                         rounded[:, piece_first - first : piece_first - first + piece_width],
                         start=(k == 0),
                         stop=(k == w_blocks - 1),
@@ -80,10 +82,9 @@ def tile_rkt_kernel(tc, emb, lab, w_in, b_in, offs, out):
             nc.sync.dma_start(out[m * P : (m + 1) * P, first : first + width], result[:])
 
         for c in range(channel_blocks - 1):
-            for early_first in range(0, entries, EARLY_WIDTH):
-                covered = [h for h, (first, width) in enumerate(pieces) if early_first <= first < early_first + EARLY_WIDTH]
-                look_up_and_project(c, c, lab_tile, early_first, EARLY_WIDTH, covered)
-                look_up_and_project(c, channel_blocks + c, not_lab_tile, early_first, EARLY_WIDTH, covered)
+            for first, width, covered in (pieces[last_piece] + ([last_piece],), (0, pieces[last_piece][0], list(range(last_piece)))):
+                look_up_and_project(c, c, lab_tile, first, width, covered)
+                look_up_and_project(c, channel_blocks + c, not_lab_tile, first, width, covered)
         c = channel_blocks - 1
         for h, (first, width) in enumerate(pieces):
             look_up_and_project(c, c, lab_tile, first, width, [h])

@@ -5,7 +5,6 @@ MULT, ADD, MAX = mybir.AluOpType.mult, mybir.AluOpType.add, mybir.AluOpType.max
 COPY, RELU = mybir.ActivationFunctionType.Copy, mybir.ActivationFunctionType.Relu
 
 P = 128
-PIECE_WIDTHS = (256, 128, 128)
 FLOPS = 2 * 512 * 256 * 512
 
 
@@ -16,10 +15,11 @@ def tile_rkt_kernel(tc, emb, lab, w_in, b_in, offs, out):
     features = out.shape[0]
     channel_blocks = channels // P
     feature_blocks = features // P
-    w_blocks = w_in.shape[0] // P
-    assert sum(PIECE_WIDTHS) == entries
-    pieces = [(sum(PIECE_WIDTHS[:h]), width) for h, width in enumerate(PIECE_WIDTHS)]
-    last_piece = len(pieces) - 1
+    U, V = 0, 1
+
+    first_half, second_half = slice(0, entries // 2), slice(entries // 2, entries)
+    third_quarter, last_quarter = slice(entries // 2, 3 * entries // 4), slice(3 * entries // 4, entries)
+    pieces = [first_half, third_quarter, last_quarter]
 
     with tc.tile_pool(name="held", bufs=1) as held, tc.psum_pool(name="psum", bufs=1) as psum:
         offsets = held.tile([P, entries // 16], U16, name="offsets")
@@ -28,70 +28,76 @@ def tile_rkt_kernel(tc, emb, lab, w_in, b_in, offs, out):
         emb_tiles = [held.tile([P, items], F32, name=f"emb{c}") for c in range(channel_blocks)]
         emb_blocks = emb.rearrange("(p c) item -> c p item", c=channel_blocks)
         lab_tile = held.tile([P, entries], F32, name="lab_tile")
-        w_tile = held.tile([P, w_blocks // channel_blocks, channel_blocks, features], BF16, name="w_tile")
+        w_tile = held.tile([P, 2, channel_blocks, features], BF16, name="w_tile")
         bias_tile = held.tile([P, feature_blocks], F32, name="bias_tile")
 
-        lab_loads = [slice(first, first + width) for first, width in [pieces[last_piece]] + pieces[:last_piece]]
-        nc.sync.dma_start(lab_tile[:, lab_loads[0]], lab[0:P, lab_loads[0]])
+        nc.sync.dma_start(lab_tile[:, first_half], lab[0:P, first_half])
         nc.sync.dma_start(emb_tiles[0][:], emb_blocks[0])
-        for columns in lab_loads[1:]:
-            nc.sync.dma_start(lab_tile[:, columns], lab[0:P, columns])
-        nc.sync.dma_start(w_tile[:], w_in.rearrange("(half p c) m -> p half c m", p=P, c=channel_blocks))
         for c in range(1, channel_blocks):
             nc.sync.dma_start(emb_tiles[c][:], emb_blocks[c])
+        nc.sync.dma_start(w_tile[:], w_in.rearrange("(half p c) m -> p half c m", p=P, c=channel_blocks))
+        nc.sync.dma_start(lab_tile[:, second_half], lab[0:P, second_half])
         with nc.allow_non_contiguous_dma(reason="one 4-byte bias to a partition"):
             nc.sync.dma_start(bias_tile[:], b_in.rearrange("(m p) one -> p (m one)", p=P))
 
         not_lab_tile = held.tile([P, entries], F32, name="not_lab_tile")
-        for columns in lab_loads:
+        for columns in (first_half, second_half):
             nc.scalar.activation(not_lab_tile[:, columns], lab_tile[:, columns], COPY, bias=1.0, scale=-1.0)
+        factors = (lab_tile, not_lab_tile)
 
-        banks = [[psum.tile([P, width], F32, name=f"bank{m}_{h}") for h, (first, width) in enumerate(pieces)] for m in range(feature_blocks)]
+        banks = [
+            [psum.tile([P, piece.stop - piece.start], F32, name=f"bank{m}_{piece.start}") for piece in pieces]
+            for m in range(feature_blocks)
+        ]
 
-        def look_up_and_project(c, k, factor, first, width, piece_numbers):
-            product = held.tile([P, width], F32, name=f"product{k}_{first}")
+        def look_up_and_project(c, half, span, rounding_engine):
+            width = span.stop - span.start
+            product = held.tile([P, width], F32, name=f"product{c}_{half}_{span.start}")
             nc.vector.tensor_tensor(
                 product[:],
-                emb_tiles[c][:].indirect(offsets[:, first // 16 : (first + width) // 16]),
-                factor[:, first : first + width],
+                emb_tiles[c][:].indirect(offsets[:, span.start // 16 : span.stop // 16]),
+                factors[half][:, span],
                 MULT,
             )
-            rounded = held.tile([P, width], BF16, name=f"rounded{k}_{first}")
-            if k == w_blocks - 1 and piece_numbers[-1] == last_piece:
+            rounded = held.tile([P, width], BF16, name=f"rounded{c}_{half}_{span.start}")
+            if rounding_engine == "vector":
                 nc.vector.tensor_copy(rounded[:], product[:])
             else:
                 nc.scalar.copy(rounded[:], product[:])
             for m in range(feature_blocks):
-                for h in piece_numbers:
-                    piece_first, piece_width = pieces[h]
-                    nc.tensor.matmul(
-                        banks[m][h][:],
-                        w_tile[:, k // channel_blocks, k % channel_blocks, m * P : (m + 1) * P],
-                        rounded[:, piece_first - first : piece_first - first + piece_width],
-                        start=(k == 0),
-                        stop=(k == w_blocks - 1),
-                    )
+                for piece, bank in zip(pieces, banks[m]):
+                    if span.start <= piece.start and piece.stop <= span.stop:
+                        nc.tensor.matmul(
+                            bank[:],
+                            w_tile[:, half, c, m * P : (m + 1) * P],
+                            rounded[:, piece.start - span.start : piece.stop - span.start],
+                            start=(c == 0 and half == U),
+                            stop=(c == channel_blocks - 1 and half == V),
+                        )
 
-        def finish(h, m):
-            first, width = pieces[h]
-            result = held.tile([P, width], F32, name=f"result{m}_{h}")
-            if m == 0:
+        def finish(h, m, engine):
+            piece = pieces[h]
+            result = held.tile([P, piece.stop - piece.start], F32, name=f"result{m}_{piece.start}")
+            if engine == "scalar":
                 nc.scalar.activation(result[:], banks[m][h][:], RELU, bias=bias_tile[:, m : m + 1])
             else:
                 nc.vector.tensor_scalar(result[:], banks[m][h][:], bias_tile[:, m : m + 1], 0.0, ADD, MAX)
-            nc.sync.dma_start(out[m * P : (m + 1) * P, first : first + width], result[:])
+            nc.sync.dma_start(out[m * P : (m + 1) * P, piece], result[:])
 
-        for c in range(channel_blocks - 1):
-            for first, width, covered in (pieces[last_piece] + ([last_piece],), (0, pieces[last_piece][0], list(range(last_piece)))):
-                look_up_and_project(c, c, lab_tile, first, width, covered)
-                look_up_and_project(c, channel_blocks + c, not_lab_tile, first, width, covered)
-        c = channel_blocks - 1
-        for h, (first, width) in enumerate(pieces):
-            look_up_and_project(c, c, lab_tile, first, width, [h])
-            look_up_and_project(c, channel_blocks + c, not_lab_tile, first, width, [h])
-            if h > 0:
-                finish(h - 1, 0)
-        for h in range(last_piece):
-            finish(h, 1)
-        for m in range(feature_blocks):
-            finish(last_piece, m)
+        for c in range(channel_blocks):
+            look_up_and_project(c, U, first_half, "scalar")
+            look_up_and_project(c, V, first_half, "scalar")
+        look_up_and_project(0, U, third_quarter, "scalar")
+        look_up_and_project(0, V, third_quarter, "scalar")
+        finish(0, 0, "scalar")
+        look_up_and_project(1, U, third_quarter, "scalar")
+        look_up_and_project(1, V, third_quarter, "scalar")
+        finish(0, 1, "scalar")
+        look_up_and_project(0, U, last_quarter, "scalar")
+        look_up_and_project(0, V, last_quarter, "scalar")
+        look_up_and_project(1, U, last_quarter, "scalar")
+        finish(1, 0, "scalar")
+        look_up_and_project(1, V, last_quarter, "vector")
+        finish(1, 1, "vector")
+        finish(2, 0, "scalar")
+        finish(2, 1, "vector")

@@ -18,6 +18,7 @@ def tile_rkt_kernel(tc, emb, lab, w_in, b_in, offs, out):
     U, V = 0, 1
 
     first_half, second_half = slice(0, entries // 2), slice(entries // 2, entries)
+    first_quarter, second_quarter = slice(0, entries // 4), slice(entries // 4, entries // 2)
     third_quarter, last_quarter = slice(entries // 2, 3 * entries // 4), slice(3 * entries // 4, entries)
     pieces = [first_half, third_quarter, last_quarter]
 
@@ -31,8 +32,9 @@ def tile_rkt_kernel(tc, emb, lab, w_in, b_in, offs, out):
         w_tile = held.tile([P, 2, channel_blocks, features], BF16, name="w_tile")
         bias_tile = held.tile([P, feature_blocks], F32, name="bias_tile")
 
-        nc.sync.dma_start(lab_tile[:, first_half], lab[0:P, first_half])
+        nc.sync.dma_start(lab_tile[:, first_quarter], lab[0:P, first_quarter])
         nc.sync.dma_start(emb_tiles[0][:], emb_blocks[0])
+        nc.sync.dma_start(lab_tile[:, second_quarter], lab[0:P, second_quarter])
         for c in range(1, channel_blocks):
             nc.sync.dma_start(emb_tiles[c][:], emb_blocks[c])
         nc.sync.dma_start(w_tile[:], w_in.rearrange("(half p c) m -> p half c m", p=P, c=channel_blocks))
@@ -50,15 +52,17 @@ def tile_rkt_kernel(tc, emb, lab, w_in, b_in, offs, out):
             for m in range(feature_blocks)
         ]
 
-        def look_up_and_project(c, half, span, rounding_engine):
+        def look_up_and_project(c, half, span, rounding_engine, steps=1):
             width = span.stop - span.start
             product = held.tile([P, width], F32, name=f"product{c}_{half}_{span.start}")
-            nc.vector.tensor_tensor(
-                product[:],
-                emb_tiles[c][:].indirect(offsets[:, span.start // 16 : span.stop // 16]),
-                factors[half][:, span],
-                MULT,
-            )
+            for first in range(span.start, span.stop, width // steps):
+                stop = first + width // steps
+                nc.vector.tensor_tensor(
+                    product[:, first - span.start : stop - span.start],
+                    emb_tiles[c][:].indirect(offsets[:, first // 16 : stop // 16]),
+                    factors[half][:, first:stop],
+                    MULT,
+                )
             rounded = held.tile([P, width], BF16, name=f"rounded{c}_{half}_{span.start}")
             if rounding_engine == "vector":
                 nc.vector.tensor_copy(rounded[:], product[:])
@@ -85,7 +89,7 @@ def tile_rkt_kernel(tc, emb, lab, w_in, b_in, offs, out):
             nc.sync.dma_start(out[m * P : (m + 1) * P, piece], result[:])
 
         for c in range(channel_blocks):
-            look_up_and_project(c, U, first_half, "scalar")
+            look_up_and_project(c, U, first_half, "scalar", steps=2 if c == 0 else 1)
             look_up_and_project(c, V, first_half, "scalar")
         look_up_and_project(0, U, third_quarter, "scalar")
         look_up_and_project(0, V, third_quarter, "scalar")

@@ -43,7 +43,7 @@ def tile_rkt_kernel(tc, emb, lab, w_in, b_in, offs, out):
             nc.sync.dma_start(bias_tile[:], b_in.rearrange("(m p) one -> p (m one)", p=P))
 
         not_lab_tile = held.tile([P, entries], F32, name="not_lab_tile")
-        for columns in (first_half, second_half):
+        for columns in (first_quarter, second_quarter, second_half):
             nc.scalar.activation(not_lab_tile[:, columns], lab_tile[:, columns], COPY, bias=1.0, scale=-1.0)
         factors = (lab_tile, not_lab_tile)
 

import concourse.mybir as mybir

F32, BF16, U16 = mybir.dt.float32, mybir.dt.bfloat16, mybir.dt.uint16
MULT, ADD, MAX = mybir.AluOpType.mult, mybir.AluOpType.add, mybir.AluOpType.max
COPY, RELU = mybir.ActivationFunctionType.Copy, mybir.ActivationFunctionType.Relu

P = 128
FLOPS = 2 * 512 * 256 * 512


def tile_rkt_kernel(tc, emb, lab, w_in, b_in, offs, out):
    nc = tc.nc
    channels, items = emb.shape
    entries = lab.shape[1]
    features = out.shape[0]
    channel_blocks = channels // P
    feature_blocks = features // P
    U, V = 0, 1

    first_half, second_half = slice(0, entries // 2), slice(entries // 2, entries)
    first_quarter, second_quarter = slice(0, entries // 4), slice(entries // 4, entries // 2)
    third_quarter, last_quarter = slice(entries // 2, 3 * entries // 4), slice(3 * entries // 4, entries)
    pieces = [first_half, third_quarter, last_quarter]

    with tc.tile_pool(name="held", bufs=1) as held, tc.psum_pool(name="psum", bufs=1) as psum:
        offsets = held.tile([P, entries // 16], U16, name="offsets")
        nc.sync.dma_start(offsets[:], offs)

        emb_tiles = [held.tile([P, items], F32, name=f"emb{c}") for c in range(channel_blocks)]
        emb_blocks = emb.rearrange("(p c) item -> c p item", c=channel_blocks)
        lab_tile = held.tile([P, entries], F32, name="lab_tile")
        w_tile = held.tile([P, 2, channel_blocks, features], BF16, name="w_tile")
        bias_tile = held.tile([P, feature_blocks], F32, name="bias_tile")

        nc.sync.dma_start(lab_tile[:, first_quarter], lab[0:P, first_quarter])
        nc.sync.dma_start(emb_tiles[0][:], emb_blocks[0])
        nc.sync.dma_start(lab_tile[:, second_quarter], lab[0:P, second_quarter])
        for c in range(1, channel_blocks):
            nc.sync.dma_start(emb_tiles[c][:], emb_blocks[c])
        nc.sync.dma_start(w_tile[:], w_in.rearrange("(half p c) m -> p half c m", p=P, c=channel_blocks))
        nc.sync.dma_start(lab_tile[:, second_half], lab[0:P, second_half])
        with nc.allow_non_contiguous_dma(reason="one 4-byte bias to a partition"):
            nc.sync.dma_start(bias_tile[:], b_in.rearrange("(m p) one -> p (m one)", p=P))

        not_lab_tile = held.tile([P, entries], F32, name="not_lab_tile")
        for columns in (first_quarter, second_quarter, second_half):
            nc.scalar.activation(not_lab_tile[:, columns], lab_tile[:, columns], COPY, bias=1.0, scale=-1.0)
        factors = (lab_tile, not_lab_tile)

        banks = [
            [psum.tile([P, piece.stop - piece.start], F32, name=f"bank{m}_{piece.start}") for piece in pieces]
            for m in range(feature_blocks)
        ]

        def look_up_and_project(c, half, span, rounding_engine, steps=1):
            width = span.stop - span.start
            product = held.tile([P, width], F32, name=f"product{c}_{half}_{span.start}")
            for first in range(span.start, span.stop, width // steps):
                stop = first + width // steps
                nc.vector.tensor_tensor(
                    product[:, first - span.start : stop - span.start],
                    emb_tiles[c][:].indirect(offsets[:, first // 16 : stop // 16]),
                    factors[half][:, first:stop],
                    MULT,
                )
            rounded = held.tile([P, width], BF16, name=f"rounded{c}_{half}_{span.start}")
            if rounding_engine == "vector":
                nc.vector.tensor_copy(rounded[:], product[:])
            else:
                nc.scalar.copy(rounded[:], product[:])
            for m in range(feature_blocks):
                for piece, bank in zip(pieces, banks[m]):
                    if span.start <= piece.start and piece.stop <= span.stop:
                        nc.tensor.matmul(
                            bank[:],
                            w_tile[:, half, c, m * P : (m + 1) * P],
                            rounded[:, piece.start - span.start : piece.stop - span.start],
                            start=(c == 0 and half == U),
                            stop=(c == channel_blocks - 1 and half == V),
                        )

        def finish(h, m, engine):
            piece = pieces[h]
            result = held.tile([P, piece.stop - piece.start], F32, name=f"result{m}_{piece.start}")
            if engine == "scalar":
                nc.scalar.activation(result[:], banks[m][h][:], RELU, bias=bias_tile[:, m : m + 1])
            else:
                nc.vector.tensor_scalar(result[:], banks[m][h][:], bias_tile[:, m : m + 1], 0.0, ADD, MAX)
            nc.sync.dma_start(out[m * P : (m + 1) * P, piece], result[:])

        for c in range(channel_blocks):
            look_up_and_project(c, U, first_half, "scalar", steps=2 if c == 0 else 1)
            look_up_and_project(c, V, first_half, "scalar")
        look_up_and_project(0, U, third_quarter, "scalar")
        look_up_and_project(0, V, third_quarter, "scalar")
        finish(0, 0, "scalar")
        look_up_and_project(1, U, third_quarter, "scalar")
        look_up_and_project(1, V, third_quarter, "scalar")
        finish(0, 1, "scalar")
        look_up_and_project(0, U, last_quarter, "scalar")
        look_up_and_project(0, V, last_quarter, "scalar")
        look_up_and_project(1, U, last_quarter, "scalar")
        finish(1, 0, "scalar")
        look_up_and_project(1, V, last_quarter, "vector")
        finish(1, 1, "vector")
        finish(2, 0, "scalar")
        finish(2, 1, "vector")
